import numpy as np
import ml_dtypes


def mxq(x, axis, fmt="e4m3"):
    dtype, down = {"e4m3": (ml_dtypes.float8_e4m3fn, 7), "e5m2": (ml_dtypes.float8_e5m2, 14)}[fmt]
    v = np.moveaxis(np.asarray(x, np.float32).astype(ml_dtypes.bfloat16).astype(np.float64), axis, -1)
    blocks = v.reshape(v.shape[:-1] + (-1, 32))
    amax = np.abs(blocks).max(-1, keepdims=True)
    byte = np.maximum(np.where(amax > 0, np.frexp(amax)[1] - 1 + 127, 0) - down, 1)
    scale = np.exp2(byte - 127.0)
    codes = (blocks / scale).astype(np.float32).astype(dtype).astype(np.float64)
    return np.moveaxis((codes * scale).reshape(v.shape), -1, axis)


WIDE = False


def mx_kscale(k):
    if not WIDE:
        return np.ones(k)
    levels = np.array([10, -10, 5, -5, 0])
    a = np.random.permutation(np.resize(levels, k // 512 * 4)).reshape(k // 512, 4)
    idx = np.arange(k)
    return np.exp2(a[idx // 512, idx % 128 // 32])


BF16 = ml_dtypes.bfloat16


def bf(x):
    return np.asarray(x, np.float32).astype(BF16)


def f64(x):
    return np.asarray(x).astype(np.float64)


L, B, E, H, D, C = 4096, 2, 1024, 2, 64, 512
F = H * D


def rope(z):
    theta = 10000.0 ** (-2.0 / D * np.arange(D // 2))
    ang = np.arange(L)[:, None] * theta[None, :]
    cos, sin = np.cos(ang), np.sin(ang)
    z2 = z.reshape(B, H, L, D // 2, 2)
    r0 = z2[..., 0] * cos - z2[..., 1] * sin
    r1 = z2[..., 0] * sin + z2[..., 1] * cos
    return np.stack([r0, r1], axis=-1).reshape(B, H, L, D)


def setup_inputs():
    s = mx_kscale(E)
    return {"x": bf(np.random.standard_normal((L, B, E)) * s),
            "w": bf(np.random.standard_normal((F, E)) / np.sqrt(E) / s[None, :]),
            "bias": bf(np.random.standard_normal(F) * 0.2)}


def reference(x, w, bias):
    y = (mxq(f64(x), 2, "e4m3") @ mxq(f64(w), 1, "e4m3").T) + f64(bias)
    z = y.reshape(L, B, H, D).transpose(1, 2, 0, 3)
    return rope(np.maximum(z, 0.0))

@@ -1,0 +1,247 @@
+import math
+
+import concourse.mybir as mybir
+from concourse.masks import make_identity
+
+F32 = mybir.dt.float32
+BF16 = mybir.dt.bfloat16
+I32 = mybir.dt.int32
+U32 = mybir.dt.uint32
+U8 = mybir.dt.uint8
+FP8X4 = mybir.dt.float8_e4m3fn_x4
+ALU = mybir.AluOpType
+ACT = mybir.ActivationFunctionType
+
+P = 128
+L, B, E, H, D = 4096, 2, 1024, 2, 64
+PAIRS = D // 2
+FLOPS = 2 * L * B * E * H * D
+
+PACK = 4
+K_PASS = P * PACK
+PASSES = E // K_PASS
+WORDS = E // 2
+TRANSPOSES = WORDS // P
+
+T = L // P
+T_GROUP = 2
+BLOCKS = T_GROUP * B
+N_GROUP = BLOCKS * P
+GROUPS = T // T_GROUP
+PLANES = B * H
+T_STORE = 8
+GROUPS_PER_STORE = T_STORE // T_GROUP
+PREFETCH = 6
+
+ROUND_MAGIC = 1.5 * 2.0**23
+
+
+def tile_weightlinearattention_pa_t_kernel(tc, x, w, bias, out):
+    nc = tc.nc
+    x_rows = x.rearrange("(p t) c k -> p t c k", t=T)
+    out_rows = out.rearrange("c h (p t) d -> p (c h) t d", t=T)
+
+    with (
+        tc.manual_schedule(),
+        tc.tile_pool(name="const", bufs=1) as const,
+        tc.tile_pool(name="loads", bufs=PREFETCH + 1) as loads,
+        tc.tile_pool(name="work", bufs=3) as work,
+        tc.psum_pool(name="flipped", bufs=4) as flipped_pool,
+        tc.psum_pool(name="sums", bufs=2) as sums_pool,
+        tc.psum_pool(name="tokens", bufs=2) as tokens_pool,
+    ):
+        x_tiles, codes_tiles, scales_tiles, grouped_tiles, relu_tiles, token_tiles = {}, {}, {}, {}, {}, {}
+        result_tiles = {}
+
+        def load(g):
+            x_sb = loads.tile([P, T_GROUP, B, E], BF16)
+            nc.sync.dma_start(out=x_sb[:], in_=x_rows[:, g * T_GROUP : (g + 1) * T_GROUP])
+            x_tiles[g] = x_sb
+
+        def flip_rows(words, grouped_words):
+            flipped = flipped_pool.tile([P, TRANSPOSES, P], F32)
+            for j in range(TRANSPOSES):
+                nc.tensor.transpose(flipped[:, j, :], words[:, j * P : (j + 1) * P], identity[:])
+            nc.scalar.copy(
+                out=grouped_words, in_=flipped[:].rearrange("p (g u) r -> p g r u", g=PASSES)
+            )
+
+        def flip_group(g):
+            words = x_tiles[g][:].bitcast(F32)
+            grouped = work.tile([P, PASSES, BLOCKS, P, PACK], BF16, align_bytes=64)
+            for t in range(T_GROUP):
+                for c in range(B):
+                    flip_rows(words[:, t, c, :], grouped[:].bitcast(F32)[:, :, t * B + c, :, :])
+            grouped_tiles[g] = grouped
+
+        def quantise(g):
+            codes = work.tile([P, PASSES * N_GROUP], U32, align_bytes=64)
+            scales = work.tile([P, PASSES * N_GROUP], U8, align_bytes=64)
+            nc.vector.quantize_mx(
+                out=codes[:].bitcast(FP8X4),
+                scales=scales[:],
+                in_=grouped_tiles[g][:].rearrange("p g b r v -> p (g b r v)"),
+            )
+            codes_tiles[g], scales_tiles[g] = codes, scales
+
+        def project(g):
+            sums = sums_pool.tile([P, N_GROUP], F32)
+            for k in range(PASSES):
+                nc.tensor.matmul_mx(
+                    out=sums[:],
+                    lhsT=w_codes[:, k * P : (k + 1) * P].bitcast(FP8X4),
+                    lhsT_scale=w_scales[:, k * P : (k + 1) * P],
+                    rhs=codes_tiles[g][:, k * N_GROUP : (k + 1) * N_GROUP].bitcast(FP8X4),
+                    rhs_scale=scales_tiles[g][:, k * N_GROUP : (k + 1) * N_GROUP],
+                    start=(k == 0),
+                    stop=(k == PASSES - 1),
+                )
+            relu = work.tile([P, N_GROUP], F32)
+            nc.scalar.activation(out=relu[:], in_=sums[:], func=ACT.Relu, bias=bias_f32[:], scale=1.0)
+            relu_tiles[g] = relu
+
+        def flip_back(g):
+            tokens = tokens_pool.tile([P, N_GROUP], F32)
+            for b in range(BLOCKS):
+                block = slice(b * P, (b + 1) * P)
+                nc.tensor.transpose(tokens[:, block], relu_tiles[g][:, block], even_then_odd[:])
+            token_tiles[g] = tokens
+
+        def rotate(g):
+            t_first = g * T_GROUP
+            shape = [P, T_GROUP, PLANES, D]
+            tokens = token_tiles[g][:].rearrange("p (t q d) -> p t q d", t=T_GROUP, q=PLANES)
+            products = work.tile([P, 2, N_GROUP], F32)
+            for a in range(2):
+                first = PAIRS * (1 - a)
+                factors = table[:, t_first : t_first + T_GROUP, first : first + D]
+                nc.vector.tensor_tensor(
+                    out=products[:, a, :].rearrange("p (t q d) -> p t q d", t=T_GROUP, q=PLANES),
+                    in0=tokens,
+                    in1=factors.unsqueeze(2).to_broadcast(shape),
+                    op=ALU.mult,
+                )
+            if g % GROUPS_PER_STORE == 0:
+                result = work.tile([P, PLANES, T_STORE, D], F32)
+                result_tiles[g // GROUPS_PER_STORE] = result
+            result = result_tiles[g // GROUPS_PER_STORE]
+            t_local = t_first % T_STORE
+            terms = products[:].rearrange(
+                "p a (t q e i) -> p e t q i a", t=T_GROUP, q=PLANES, e=2
+            )
+            nc.vector.tensor_tensor(
+                out=result[:, :, t_local : t_local + T_GROUP, :].rearrange(
+                    "p q t (i a) -> p t q i a", a=2
+                ),
+                in0=terms[:, 0],
+                in1=terms[:, 1],
+                op=ALU.add,
+            )
+            if g % GROUPS_PER_STORE == GROUPS_PER_STORE - 1:
+                t_done = t_first + T_GROUP
+                nc.sync.dma_start(out=out_rows[:, :, t_done - T_STORE : t_done, :], in_=result[:])
+
+        w_sb = const.tile([P, E], BF16)
+        nc.sync.dma_start(out=w_sb[:], in_=w)
+        for g in range(PREFETCH):
+            load(g)
+        bias_bf16 = const.tile([P, 1], BF16)
+        nc.scalar.dma_start(out=bias_bf16[:], in_=bias.rearrange("(f o) -> f o", o=1))
+
+        identity = const.tile([P, P], F32)
+        make_identity(nc, identity[:])
+        position_i32 = const.tile([P, T], I32)
+        nc.gpsimd.iota(position_i32[:], pattern=[[1, T]], base=0, channel_multiplier=T)
+
+        zero = const.tile([P, 1], F32)
+        nc.vector.memset(zero[:], 0.0)
+        first_sine = const.tile([P, 1], F32)
+        nc.scalar.activation(out=first_sine[:], in_=zero[:], func=ACT.Sin)
+
+        position = const.tile([P, T], F32)
+        nc.vector.tensor_copy(out=position[:], in_=position_i32[:])
+        turns = const.tile([P, PAIRS, T], F32)
+        for i in range(PAIRS):
+            theta = 10000.0 ** (-2.0 * i / D)
+            nc.vector.tensor_scalar_mul(
+                out=turns[:, i, :], in0=position[:], scalar1=theta / (2 * math.pi)
+            )
+        whole_turns = const.tile([P, PAIRS, T], F32)
+        nc.vector.tensor_scalar(
+            out=whole_turns[:],
+            in0=turns[:],
+            scalar1=ROUND_MAGIC,
+            scalar2=ROUND_MAGIC,
+            op0=ALU.add,
+            op1=ALU.subtract,
+        )
+        fraction = const.tile([P, T * PAIRS], F32)
+        nc.vector.tensor_tensor(
+            out=fraction[:].rearrange("p (t i) -> p t i", t=T),
+            in0=turns[:].rearrange("p i t -> p t i"),
+            in1=whole_turns[:].rearrange("p i t -> p t i"),
+            op=ALU.subtract,
+        )
+        quarter_less = const.tile([P, T * PAIRS], F32)
+        nc.vector.scalar_tensor_tensor(
+            out=quarter_less[:],
+            in0=fraction[:],
+            scalar=-1.0,
+            in1=fraction[:],
+            op0=ALU.mult,
+            op1=ALU.min,
+        )
+        nc.vector.tensor_scalar_add(out=quarter_less[:], in0=quarter_less[:], scalar1=0.25)
+
+        even_then_odd = const.tile([P, P], F32)
+        nc.vector.tensor_copy(
+            out=even_then_odd[:].rearrange("p (h e i) -> p h e i", h=H, e=2),
+            in_=identity[:].rearrange("p (h i e) -> p h e i", h=H, e=2),
+        )
+        bias_f32 = const.tile([P, 1], F32)
+        nc.vector.tensor_copy(out=bias_f32[:], in_=bias_bf16[:])
+
+        w_grouped = const.tile([P, PASSES, P, PACK], BF16, align_bytes=64)
+        flip_rows(w_sb[:].bitcast(F32), w_grouped[:].bitcast(F32))
+        w_codes = const.tile([P, PASSES * P], U32, align_bytes=64)
+        w_scales = const.tile([P, PASSES * P], U8, align_bytes=64)
+        nc.vector.quantize_mx(
+            out=w_codes[:].bitcast(FP8X4),
+            scales=w_scales[:],
+            in_=w_grouped[:].rearrange("p g r v -> p (g r v)"),
+        )
+
+        flip_group(0)
+        table = const.tile([P, T, 3 * PAIRS], F32)
+        by_position = "p (t i) -> p t i"
+        nc.scalar.activation(
+            out=table[:, :, 0:PAIRS],
+            in_=fraction[:].rearrange(by_position, t=T),
+            func=ACT.Sin,
+            scale=2 * math.pi,
+        )
+        nc.scalar.activation(
+            out=table[:, :, PAIRS : 2 * PAIRS],
+            in_=quarter_less[:].rearrange(by_position, t=T),
+            func=ACT.Sin,
+            scale=2 * math.pi,
+        )
+        nc.scalar.activation(
+            out=table[:, :, 2 * PAIRS : 3 * PAIRS],
+            in_=fraction[:].rearrange(by_position, t=T),
+            func=ACT.Sin,
+            scale=-2 * math.pi,
+        )
+
+        for r in range(1, GROUPS + 3):
+            if r - 1 + PREFETCH < GROUPS:
+                load(r - 1 + PREFETCH)
+            if r < GROUPS:
+                flip_group(r)
+            if 0 <= r - 2 < GROUPS:
+                flip_back(r - 2)
+            if r - 1 < GROUPS:
+                quantise(r - 1)
+                project(r - 1)
+            if r - 3 >= 0:
+                rotate(r - 3)

@@ -31,6 +31,7 @@ GROUPS = T // T_GROUP
 PLANES = B * H
 T_STORE = 8
 GROUPS_PER_STORE = T_STORE // T_GROUP
+VECTOR_BLOCKS = 1
 PREFETCH = 6
 
 ROUND_MAGIC = 1.5 * 2.0**23
@@ -58,20 +59,27 @@ def tile_weightlinearattention_pa_t_kernel(tc, x, w, bias, out):
             nc.sync.dma_start(out=x_sb[:], in_=x_rows[:, g * T_GROUP : (g + 1) * T_GROUP])
             x_tiles[g] = x_sb
 
-        def flip_rows(words, grouped_words):
+        def flip_rows(words, grouped_words, by_vector):
             flipped = flipped_pool.tile([P, TRANSPOSES, P], F32)
             for j in range(TRANSPOSES):
                 nc.tensor.transpose(flipped[:, j, :], words[:, j * P : (j + 1) * P], identity[:])
-            nc.scalar.copy(
-                out=grouped_words, in_=flipped[:].rearrange("p (g u) r -> p g r u", g=PASSES)
-            )
+            side_by_side = flipped[:].rearrange("p (g u) r -> p g r u", g=PASSES)
+            if by_vector:
+                nc.vector.tensor_copy(out=grouped_words, in_=side_by_side)
+            else:
+                nc.scalar.copy(out=grouped_words, in_=side_by_side)
 
         def flip_group(g):
             words = x_tiles[g][:].bitcast(F32)
             grouped = work.tile([P, PASSES, BLOCKS, P, PACK], BF16, align_bytes=64)
             for t in range(T_GROUP):
                 for c in range(B):
-                    flip_rows(words[:, t, c, :], grouped[:].bitcast(F32)[:, :, t * B + c, :, :])
+                    b = t * B + c
+                    flip_rows(
+                        words[:, t, c, :],
+                        grouped[:].bitcast(F32)[:, :, b, :, :],
+                        by_vector=(b < VECTOR_BLOCKS),
+                    )
             grouped_tiles[g] = grouped
 
         def quantise(g):
@@ -129,7 +137,7 @@ def tile_weightlinearattention_pa_t_kernel(tc, x, w, bias, out):
             terms = products[:].rearrange(
                 "p a (t q e i) -> p e t q i a", t=T_GROUP, q=PLANES, e=2
             )
-            nc.vector.tensor_tensor(
+            nc.gpsimd.tensor_tensor(
                 out=result[:, :, t_local : t_local + T_GROUP, :].rearrange(
                     "p q t (i a) -> p t q i a", a=2
                 ),
@@ -202,7 +210,7 @@ def tile_weightlinearattention_pa_t_kernel(tc, x, w, bias, out):
         nc.vector.tensor_copy(out=bias_f32[:], in_=bias_bf16[:])
 
         w_grouped = const.tile([P, PASSES, P, PACK], BF16, align_bytes=64)
-        flip_rows(w_sb[:].bitcast(F32), w_grouped[:].bitcast(F32))
+        flip_rows(w_sb[:].bitcast(F32), w_grouped[:].bitcast(F32), by_vector=False)
         w_codes = const.tile([P, PASSES * P], U32, align_bytes=64)
         w_scales = const.tile([P, PASSES * P], U8, align_bytes=64)
         nc.vector.quantize_mx(
@@ -236,12 +244,13 @@ def tile_weightlinearattention_pa_t_kernel(tc, x, w, bias, out):
         for r in range(1, GROUPS + 3):
             if r - 1 + PREFETCH < GROUPS:
                 load(r - 1 + PREFETCH)
+            if r - 1 < GROUPS:
+                quantise(r - 1)
             if r < GROUPS:
                 flip_group(r)
             if 0 <= r - 2 < GROUPS:
                 flip_back(r - 2)
             if r - 1 < GROUPS:
-                quantise(r - 1)
                 project(r - 1)
             if r - 3 >= 0:
                 rotate(r - 3)

@@ -24,17 +24,20 @@ WORDS = E // 2
 TRANSPOSES = WORDS // P
 
 T = L // P
-T_GROUP = 2
-BLOCKS = T_GROUP * B
-N_GROUP = BLOCKS * P
-GROUPS = T // T_GROUP
+GROUP_T = (1, 1) + (2,) * 14 + (1, 1)
+GROUPS = len(GROUP_T)
+FIRST_T = tuple(sum(GROUP_T[:g]) for g in range(GROUPS))
+N_MAX = max(GROUP_T) * B * P
 PLANES = B * H
-T_STORE = 8
-GROUPS_PER_STORE = T_STORE // T_GROUP
+STORE_T = (8, 8, 8, 4, 2, 1, 1)
+STORE_ENDS = tuple(sum(STORE_T[: s + 1]) for s in range(len(STORE_T)))
 VECTOR_BLOCKS = 1
-PREFETCH = 6
+PREFETCH = 7
+TABLE_T = (8, 12, 12)
+TABLE_FIRST = tuple(sum(TABLE_T[:c]) for c in range(len(TABLE_T)))
 
 ROUND_MAGIC = 1.5 * 2.0**23
+DIRECT_THETAS = 8
 
 
 def tile_weightlinearattention_pa_t_kernel(tc, x, w, bias, out):
@@ -47,16 +50,17 @@ def tile_weightlinearattention_pa_t_kernel(tc, x, w, bias, out):
         tc.tile_pool(name="const", bufs=1) as const,
         tc.tile_pool(name="loads", bufs=PREFETCH + 1) as loads,
         tc.tile_pool(name="work", bufs=3) as work,
+        tc.tile_pool(name="results", bufs=5) as results,
         tc.psum_pool(name="flipped", bufs=4) as flipped_pool,
         tc.psum_pool(name="sums", bufs=2) as sums_pool,
         tc.psum_pool(name="tokens", bufs=2) as tokens_pool,
     ):
         x_tiles, codes_tiles, scales_tiles, grouped_tiles, relu_tiles, token_tiles = {}, {}, {}, {}, {}, {}
-        result_tiles = {}
+        result_tiles, fraction_tiles, quarter_tiles = {}, {}, {}
 
         def load(g):
-            x_sb = loads.tile([P, T_GROUP, B, E], BF16)
-            nc.sync.dma_start(out=x_sb[:], in_=x_rows[:, g * T_GROUP : (g + 1) * T_GROUP])
+            x_sb = loads.tile([P, GROUP_T[g], B, E], BF16)
+            nc.sync.dma_start(out=x_sb[:], in_=x_rows[:, FIRST_T[g] : FIRST_T[g] + GROUP_T[g]])
             x_tiles[g] = x_sb
 
         def flip_rows(words, grouped_words, by_vector):
@@ -71,20 +75,22 @@ def tile_weightlinearattention_pa_t_kernel(tc, x, w, bias, out):
 
         def flip_group(g):
             words = x_tiles[g][:].bitcast(F32)
-            grouped = work.tile([P, PASSES, BLOCKS, P, PACK], BF16, align_bytes=64)
-            for t in range(T_GROUP):
+            blocks = GROUP_T[g] * B
+            grouped = work.tile([P, PASSES, blocks, P, PACK], BF16, align_bytes=64)
+            for t in range(GROUP_T[g]):
                 for c in range(B):
                     b = t * B + c
                     flip_rows(
                         words[:, t, c, :],
                         grouped[:].bitcast(F32)[:, :, b, :, :],
-                        by_vector=(b < VECTOR_BLOCKS),
+                        by_vector=(b < VECTOR_BLOCKS and GROUP_T[g] > 1),
                     )
             grouped_tiles[g] = grouped
 
         def quantise(g):
-            codes = work.tile([P, PASSES * N_GROUP], U32, align_bytes=64)
-            scales = work.tile([P, PASSES * N_GROUP], U8, align_bytes=64)
+            n = GROUP_T[g] * B * P
+            codes = work.tile([P, PASSES * n], U32, align_bytes=64)
+            scales = work.tile([P, PASSES * n], U8, align_bytes=64)
             nc.vector.quantize_mx(
                 out=codes[:].bitcast(FP8X4),
                 scales=scales[:],
@@ -93,61 +99,107 @@ def tile_weightlinearattention_pa_t_kernel(tc, x, w, bias, out):
             codes_tiles[g], scales_tiles[g] = codes, scales
 
         def project(g):
-            sums = sums_pool.tile([P, N_GROUP], F32)
+            n = GROUP_T[g] * B * P
+            sums = sums_pool.tile([P, N_MAX], F32)
             for k in range(PASSES):
                 nc.tensor.matmul_mx(
-                    out=sums[:],
+                    out=sums[:, :n],
                     lhsT=w_codes[:, k * P : (k + 1) * P].bitcast(FP8X4),
                     lhsT_scale=w_scales[:, k * P : (k + 1) * P],
-                    rhs=codes_tiles[g][:, k * N_GROUP : (k + 1) * N_GROUP].bitcast(FP8X4),
-                    rhs_scale=scales_tiles[g][:, k * N_GROUP : (k + 1) * N_GROUP],
+                    rhs=codes_tiles[g][:, k * n : (k + 1) * n].bitcast(FP8X4),
+                    rhs_scale=scales_tiles[g][:, k * n : (k + 1) * n],
                     start=(k == 0),
                     stop=(k == PASSES - 1),
                 )
-            relu = work.tile([P, N_GROUP], F32)
-            nc.scalar.activation(out=relu[:], in_=sums[:], func=ACT.Relu, bias=bias_f32[:], scale=1.0)
+            relu = work.tile([P, n], F32)
+            nc.scalar.activation(out=relu[:], in_=sums[:, :n], func=ACT.Relu, bias=bias_f32[:], scale=1.0)
             relu_tiles[g] = relu
 
         def flip_back(g):
-            tokens = tokens_pool.tile([P, N_GROUP], F32)
-            for b in range(BLOCKS):
+            tokens = tokens_pool.tile([P, N_MAX], F32)
+            for b in range(GROUP_T[g] * B):
                 block = slice(b * P, (b + 1) * P)
                 nc.tensor.transpose(tokens[:, block], relu_tiles[g][:, block], even_then_odd[:])
             token_tiles[g] = tokens
 
-        def rotate(g):
-            t_first = g * T_GROUP
-            shape = [P, T_GROUP, PLANES, D]
-            tokens = token_tiles[g][:].rearrange("p (t q d) -> p t q d", t=T_GROUP, q=PLANES)
-            products = work.tile([P, 2, N_GROUP], F32)
+        def rotate(g, add_engine):
+            first, size = FIRST_T[g], GROUP_T[g]
+            n = size * B * P
+            shape = [P, size, PLANES, D]
+            tokens = token_tiles[g][:, :n].rearrange("p (t q d) -> p t q d", t=size, q=PLANES)
+            products = work.tile([P, 2, n], F32)
             for a in range(2):
-                first = PAIRS * (1 - a)
-                factors = table[:, t_first : t_first + T_GROUP, first : first + D]
+                column = PAIRS * (1 - a)
+                factors = table[:, first : first + size, column : column + D]
                 nc.vector.tensor_tensor(
-                    out=products[:, a, :].rearrange("p (t q d) -> p t q d", t=T_GROUP, q=PLANES),
+                    out=products[:, a, :].rearrange("p (t q d) -> p t q d", t=size, q=PLANES),
                     in0=tokens,
                     in1=factors.unsqueeze(2).to_broadcast(shape),
                     op=ALU.mult,
                 )
-            if g % GROUPS_PER_STORE == 0:
-                result = work.tile([P, PLANES, T_STORE, D], F32)
-                result_tiles[g // GROUPS_PER_STORE] = result
-            result = result_tiles[g // GROUPS_PER_STORE]
-            t_local = t_first % T_STORE
-            terms = products[:].rearrange(
-                "p a (t q e i) -> p e t q i a", t=T_GROUP, q=PLANES, e=2
-            )
-            nc.gpsimd.tensor_tensor(
-                out=result[:, :, t_local : t_local + T_GROUP, :].rearrange(
-                    "p q t (i a) -> p t q i a", a=2
-                ),
+            s = min(i for i in range(len(STORE_T)) if first < STORE_ENDS[i])
+            store_first = STORE_ENDS[s] - STORE_T[s]
+            if first == store_first:
+                result = results.tile([P, PLANES, STORE_T[s], D], F32)
+                result_tiles[s] = result
+            result = result_tiles[s]
+            local = first - store_first
+            terms = products[:].rearrange("p a (t q e i) -> p e t q i a", t=size, q=PLANES, e=2)
+            add_engine.tensor_tensor(
+                out=result[:, :, local : local + size, :].rearrange("p q t (i a) -> p t q i a", a=2),
                 in0=terms[:, 0],
                 in1=terms[:, 1],
                 op=ALU.add,
             )
-            if g % GROUPS_PER_STORE == GROUPS_PER_STORE - 1:
-                t_done = t_first + T_GROUP
-                nc.sync.dma_start(out=out_rows[:, :, t_done - T_STORE : t_done, :], in_=result[:])
+            if first + size == STORE_ENDS[s]:
+                nc.sync.dma_start(out=out_rows[:, :, store_first : STORE_ENDS[s], :], in_=result[:])
+
+        def angles(c):
+            first, size = TABLE_FIRST[c], TABLE_T[c]
+            shape = [P, size, PAIRS]
+            turns = work.tile([P, size, PAIRS], F32)
+            nc.vector.tensor_tensor(
+                out=turns[:],
+                in0=position[:, first : first + size].unsqueeze(2).to_broadcast(shape),
+                in1=theta[:].unsqueeze(1).to_broadcast(shape),
+                op=ALU.mult,
+            )
+            whole_turns = work.tile([P, size, PAIRS], F32)
+            nc.vector.tensor_scalar(
+                out=whole_turns[:],
+                in0=turns[:],
+                scalar1=ROUND_MAGIC,
+                scalar2=ROUND_MAGIC,
+                op0=ALU.add,
+                op1=ALU.subtract,
+            )
+            fraction = work.tile([P, size, PAIRS], F32)
+            nc.vector.tensor_tensor(out=fraction[:], in0=turns[:], in1=whole_turns[:], op=ALU.subtract)
+            quarter_less = work.tile([P, size, PAIRS], F32)
+            nc.vector.scalar_tensor_tensor(
+                out=quarter_less[:],
+                in0=fraction[:],
+                scalar=-1.0,
+                in1=fraction[:],
+                op0=ALU.mult,
+                op1=ALU.min,
+            )
+            nc.vector.tensor_scalar_add(out=quarter_less[:], in0=quarter_less[:], scalar1=0.25)
+            fraction_tiles[c], quarter_tiles[c] = fraction, quarter_less
+
+        def sines(c):
+            part = slice(TABLE_FIRST[c], TABLE_FIRST[c] + TABLE_T[c])
+            for column, source, sign in (
+                (0, fraction_tiles[c], 1.0),
+                (2 * PAIRS, fraction_tiles[c], -1.0),
+                (PAIRS, quarter_tiles[c], 1.0),
+            ):
+                nc.scalar.activation(
+                    out=table[:, part, column : column + PAIRS],
+                    in_=source[:],
+                    func=ACT.Sin,
+                    scale=sign * 2 * math.pi,
+                )
 
         w_sb = const.tile([P, E], BF16)
         nc.sync.dma_start(out=w_sb[:], in_=w)
@@ -156,50 +208,33 @@ def tile_weightlinearattention_pa_t_kernel(tc, x, w, bias, out):
         bias_bf16 = const.tile([P, 1], BF16)
         nc.scalar.dma_start(out=bias_bf16[:], in_=bias.rearrange("(f o) -> f o", o=1))
 
-        identity = const.tile([P, P], F32)
-        make_identity(nc, identity[:])
         position_i32 = const.tile([P, T], I32)
         nc.gpsimd.iota(position_i32[:], pattern=[[1, T]], base=0, channel_multiplier=T)
+        identity = const.tile([P, P], F32)
+        make_identity(nc, identity[:])
 
-        zero = const.tile([P, 1], F32)
-        nc.vector.memset(zero[:], 0.0)
+        one = const.tile([P, 1], F32)
+        nc.vector.memset(one[:], 1.0)
         first_sine = const.tile([P, 1], F32)
-        nc.scalar.activation(out=first_sine[:], in_=zero[:], func=ACT.Sin)
+        nc.scalar.activation(out=first_sine[:], in_=one[:], func=ACT.Sin)
 
+        theta = const.tile([P, PAIRS], F32)
+        for i in range(DIRECT_THETAS):
+            nc.vector.tensor_scalar_mul(
+                out=theta[:, i : i + 1], in0=one[:], scalar1=10000.0 ** (-2.0 * i / D) / (2 * math.pi)
+            )
+        made = DIRECT_THETAS
+        while made < PAIRS:
+            nc.vector.tensor_scalar_mul(
+                out=theta[:, made : 2 * made], in0=theta[:, :made], scalar1=10000.0 ** (-2.0 * made / D)
+            )
+            made = 2 * made
         position = const.tile([P, T], F32)
         nc.vector.tensor_copy(out=position[:], in_=position_i32[:])
-        turns = const.tile([P, PAIRS, T], F32)
-        for i in range(PAIRS):
-            theta = 10000.0 ** (-2.0 * i / D)
-            nc.vector.tensor_scalar_mul(
-                out=turns[:, i, :], in0=position[:], scalar1=theta / (2 * math.pi)
-            )
-        whole_turns = const.tile([P, PAIRS, T], F32)
-        nc.vector.tensor_scalar(
-            out=whole_turns[:],
-            in0=turns[:],
-            scalar1=ROUND_MAGIC,
-            scalar2=ROUND_MAGIC,
-            op0=ALU.add,
-            op1=ALU.subtract,
-        )
-        fraction = const.tile([P, T * PAIRS], F32)
-        nc.vector.tensor_tensor(
-            out=fraction[:].rearrange("p (t i) -> p t i", t=T),
-            in0=turns[:].rearrange("p i t -> p t i"),
-            in1=whole_turns[:].rearrange("p i t -> p t i"),
-            op=ALU.subtract,
-        )
-        quarter_less = const.tile([P, T * PAIRS], F32)
-        nc.vector.scalar_tensor_tensor(
-            out=quarter_less[:],
-            in0=fraction[:],
-            scalar=-1.0,
-            in1=fraction[:],
-            op0=ALU.mult,
-            op1=ALU.min,
-        )
-        nc.vector.tensor_scalar_add(out=quarter_less[:], in0=quarter_less[:], scalar1=0.25)
+        table = const.tile([P, T, 3 * PAIRS], F32)
+        angles(0)
+        sines(0)
+        angles(1)
 
         even_then_odd = const.tile([P, P], F32)
         nc.vector.tensor_copy(
@@ -218,28 +253,7 @@ def tile_weightlinearattention_pa_t_kernel(tc, x, w, bias, out):
             scales=w_scales[:],
             in_=w_grouped[:].rearrange("p g r v -> p (g r v)"),
         )
-
         flip_group(0)
-        table = const.tile([P, T, 3 * PAIRS], F32)
-        by_position = "p (t i) -> p t i"
-        nc.scalar.activation(
-            out=table[:, :, 0:PAIRS],
-            in_=fraction[:].rearrange(by_position, t=T),
-            func=ACT.Sin,
-            scale=2 * math.pi,
-        )
-        nc.scalar.activation(
-            out=table[:, :, PAIRS : 2 * PAIRS],
-            in_=quarter_less[:].rearrange(by_position, t=T),
-            func=ACT.Sin,
-            scale=2 * math.pi,
-        )
-        nc.scalar.activation(
-            out=table[:, :, 2 * PAIRS : 3 * PAIRS],
-            in_=fraction[:].rearrange(by_position, t=T),
-            func=ACT.Sin,
-            scale=-2 * math.pi,
-        )
 
         for r in range(1, GROUPS + 3):
             if r - 1 + PREFETCH < GROUPS:
@@ -253,4 +267,8 @@ def tile_weightlinearattention_pa_t_kernel(tc, x, w, bias, out):
             if r - 1 < GROUPS:
                 project(r - 1)
             if r - 3 >= 0:
-                rotate(r - 3)
+                rotate(r - 3, nc.vector if r >= GROUPS + 1 else nc.gpsimd)
+            if r == 1:
+                angles(2)
+            if 1 <= r - 1 < len(TABLE_T):
+                sines(r - 1)

@@ -51,6 +51,7 @@ def tile_weightlinearattention_pa_t_kernel(tc, x, w, bias, out):
         tc.tile_pool(name="loads", bufs=PREFETCH + 1) as loads,
         tc.tile_pool(name="work", bufs=3) as work,
         tc.tile_pool(name="results", bufs=5) as results,
+        tc.tile_pool(name="grouped", bufs=4) as groupeds,
         tc.psum_pool(name="flipped", bufs=4) as flipped_pool,
         tc.psum_pool(name="sums", bufs=2) as sums_pool,
         tc.psum_pool(name="tokens", bufs=2) as tokens_pool,
@@ -76,14 +77,14 @@ def tile_weightlinearattention_pa_t_kernel(tc, x, w, bias, out):
         def flip_group(g):
             words = x_tiles[g][:].bitcast(F32)
             blocks = GROUP_T[g] * B
-            grouped = work.tile([P, PASSES, blocks, P, PACK], BF16, align_bytes=64)
+            grouped = groupeds.tile([P, PASSES, blocks, P, PACK], BF16, align_bytes=64)
             for t in range(GROUP_T[g]):
                 for c in range(B):
                     b = t * B + c
                     flip_rows(
                         words[:, t, c, :],
                         grouped[:].bitcast(F32)[:, :, b, :, :],
-                        by_vector=(b < VECTOR_BLOCKS and GROUP_T[g] > 1),
+                        by_vector=((b < VECTOR_BLOCKS and GROUP_T[g] > 1)),
                     )
             grouped_tiles[g] = grouped
 
@@ -253,22 +254,22 @@ def tile_weightlinearattention_pa_t_kernel(tc, x, w, bias, out):
             scales=w_scales[:],
             in_=w_grouped[:].rearrange("p g r v -> p (g r v)"),
         )
-        flip_group(0)
-
-        for r in range(1, GROUPS + 3):
-            if r - 1 + PREFETCH < GROUPS:
+        for r in range(GROUPS + 4):
+            if 0 < r <= GROUPS - PREFETCH:
                 load(r - 1 + PREFETCH)
-            if r - 1 < GROUPS:
-                quantise(r - 1)
+            if 0 <= r - 2 < GROUPS:
+                quantise(r - 2)
             if r < GROUPS:
                 flip_group(r)
+            if 0 <= r - 3 < GROUPS:
+                flip_back(r - 3)
             if 0 <= r - 2 < GROUPS:
-                flip_back(r - 2)
-            if r - 1 < GROUPS:
-                project(r - 1)
-            if r - 3 >= 0:
-                rotate(r - 3, nc.vector if r >= GROUPS + 1 else nc.gpsimd)
+                project(r - 2)
+            if r - 4 >= 0:
+                rotate(r - 4, nc.vector if r - 4 >= GROUPS - 4 else nc.gpsimd)
             if r == 1:
+                sines(1)
+            if r == 2:
                 angles(2)
-            if 1 <= r - 1 < len(TABLE_T):
-                sines(r - 1)
+            if r == 3:
+                sines(2)

@@ -31,10 +31,12 @@ N_MAX = max(GROUP_T) * B * P
 PLANES = B * H
 STORE_T = (8, 8, 8, 4, 2, 1, 1)
 STORE_ENDS = tuple(sum(STORE_T[: s + 1]) for s in range(len(STORE_T)))
-VECTOR_BLOCKS = 1
 PREFETCH = 7
-TABLE_T = (8, 12, 12)
+TABLE_T = (8, 8, 16)
 TABLE_FIRST = tuple(sum(TABLE_T[:c]) for c in range(len(TABLE_T)))
+
+SIN, COS, MINUS_SIN = 0, PAIRS, 2 * PAIRS
+GPSIMD_ADDS = GROUPS - 6
 
 ROUND_MAGIC = 1.5 * 2.0**23
 DIRECT_THETAS = 8
@@ -57,7 +59,7 @@ def tile_weightlinearattention_pa_t_kernel(tc, x, w, bias, out):
         tc.psum_pool(name="tokens", bufs=2) as tokens_pool,
     ):
         x_tiles, codes_tiles, scales_tiles, grouped_tiles, relu_tiles, token_tiles = {}, {}, {}, {}, {}, {}
-        result_tiles, fraction_tiles, quarter_tiles = {}, {}, {}
+        result_tiles, turns_tiles, whole_tiles, fraction_tiles, folded_tiles = {}, {}, {}, {}, {}
 
         def load(g):
             x_sb = loads.tile([P, GROUP_T[g], B, E], BF16)
@@ -84,7 +86,7 @@ def tile_weightlinearattention_pa_t_kernel(tc, x, w, bias, out):
                     flip_rows(
                         words[:, t, c, :],
                         grouped[:].bitcast(F32)[:, :, b, :, :],
-                        by_vector=((b < VECTOR_BLOCKS and GROUP_T[g] > 1)),
+                        by_vector=(b == 0 and GROUP_T[g] == 2),
                     )
             grouped_tiles[g] = grouped
 
@@ -130,7 +132,7 @@ def tile_weightlinearattention_pa_t_kernel(tc, x, w, bias, out):
             tokens = token_tiles[g][:, :n].rearrange("p (t q d) -> p t q d", t=size, q=PLANES)
             products = work.tile([P, 2, n], F32)
             for a in range(2):
-                column = PAIRS * (1 - a)
+                column = (COS, SIN)[a]
                 factors = table[:, first : first + size, column : column + D]
                 nc.vector.tensor_tensor(
                     out=products[:, a, :].rearrange("p (t q d) -> p t q d", t=size, q=PLANES),
@@ -155,52 +157,78 @@ def tile_weightlinearattention_pa_t_kernel(tc, x, w, bias, out):
             if first + size == STORE_ENDS[s]:
                 nc.sync.dma_start(out=out_rows[:, :, store_first : STORE_ENDS[s], :], in_=result[:])
 
-        def angles(c):
-            first, size = TABLE_FIRST[c], TABLE_T[c]
-            shape = [P, size, PAIRS]
-            turns = work.tile([P, size, PAIRS], F32)
-            nc.vector.tensor_tensor(
-                out=turns[:],
-                in0=position[:, first : first + size].unsqueeze(2).to_broadcast(shape),
-                in1=theta[:].unsqueeze(1).to_broadcast(shape),
-                op=ALU.mult,
-            )
-            whole_turns = work.tile([P, size, PAIRS], F32)
-            nc.vector.tensor_scalar(
-                out=whole_turns[:],
-                in0=turns[:],
-                scalar1=ROUND_MAGIC,
-                scalar2=ROUND_MAGIC,
-                op0=ALU.add,
-                op1=ALU.subtract,
-            )
-            fraction = work.tile([P, size, PAIRS], F32)
-            nc.vector.tensor_tensor(out=fraction[:], in0=turns[:], in1=whole_turns[:], op=ALU.subtract)
-            quarter_less = work.tile([P, size, PAIRS], F32)
-            nc.vector.scalar_tensor_tensor(
-                out=quarter_less[:],
-                in0=fraction[:],
-                scalar=-1.0,
-                in1=fraction[:],
-                op0=ALU.mult,
-                op1=ALU.min,
-            )
-            nc.vector.tensor_scalar_add(out=quarter_less[:], in0=quarter_less[:], scalar1=0.25)
-            fraction_tiles[c], quarter_tiles[c] = fraction, quarter_less
-
-        def sines(c):
-            part = slice(TABLE_FIRST[c], TABLE_FIRST[c] + TABLE_T[c])
-            for column, source, sign in (
-                (0, fraction_tiles[c], 1.0),
-                (2 * PAIRS, fraction_tiles[c], -1.0),
-                (PAIRS, quarter_tiles[c], 1.0),
-            ):
-                nc.scalar.activation(
-                    out=table[:, part, column : column + PAIRS],
-                    in_=source[:],
-                    func=ACT.Sin,
-                    scale=sign * 2 * math.pi,
+        def angles(parts):
+            for c in parts:
+                first, size = TABLE_FIRST[c], TABLE_T[c]
+                shape = [P, size, PAIRS]
+                turns = work.tile([P, size, PAIRS], F32)
+                nc.vector.tensor_tensor(
+                    out=turns[:],
+                    in0=position[:, first : first + size].unsqueeze(2).to_broadcast(shape),
+                    in1=theta[:].unsqueeze(1).to_broadcast(shape),
+                    op=ALU.mult,
                 )
+                turns_tiles[c] = turns
+            for c in parts:
+                whole_turns = work.tile([P, TABLE_T[c], PAIRS], F32)
+                nc.vector.tensor_scalar(
+                    out=whole_turns[:],
+                    in0=turns_tiles[c][:],
+                    scalar1=ROUND_MAGIC,
+                    scalar2=ROUND_MAGIC,
+                    op0=ALU.add,
+                    op1=ALU.subtract,
+                )
+                whole_tiles[c] = whole_turns
+            for c in parts:
+                fraction = work.tile([P, TABLE_T[c], PAIRS], F32)
+                nc.vector.tensor_tensor(
+                    out=fraction[:], in0=turns_tiles[c][:], in1=whole_tiles[c][:], op=ALU.subtract
+                )
+                fraction_tiles[c] = fraction
+            for c in parts:
+                folded = work.tile([P, TABLE_T[c], PAIRS], F32)
+                nc.vector.scalar_tensor_tensor(
+                    out=folded[:],
+                    in0=fraction_tiles[c][:],
+                    scalar=-1.0,
+                    in1=fraction_tiles[c][:],
+                    op0=ALU.mult,
+                    op1=ALU.min,
+                )
+                folded_tiles[c] = folded
+
+        def table_part(c, column):
+            return table[:, TABLE_FIRST[c] : TABLE_FIRST[c] + TABLE_T[c], column : column + PAIRS]
+
+        def sine(c):
+            nc.scalar.activation(
+                out=table_part(c, SIN), in_=fraction_tiles[c][:], func=ACT.Sin, scale=2 * math.pi
+            )
+
+        def cosine(c):
+            nc.scalar.activation(
+                out=table_part(c, COS),
+                in_=folded_tiles[c][:],
+                func=ACT.Sin,
+                bias=quarter_turn[:],
+                scale=2 * math.pi,
+            )
+
+        def minus_sine(c):
+            nc.scalar.activation(
+                out=table_part(c, MINUS_SIN), in_=fraction_tiles[c][:], func=ACT.Sin, scale=-2 * math.pi
+            )
+
+        def negate(c):
+            nc.gpsimd.tensor_scalar(
+                out=table_part(c, MINUS_SIN),
+                in0=table_part(c, SIN),
+                scalar1=-1.0,
+                scalar2=0.0,
+                op0=ALU.mult,
+                op1=ALU.add,
+            )
 
         w_sb = const.tile([P, E], BF16)
         nc.sync.dma_start(out=w_sb[:], in_=w)
@@ -232,18 +260,21 @@ def tile_weightlinearattention_pa_t_kernel(tc, x, w, bias, out):
             made = 2 * made
         position = const.tile([P, T], F32)
         nc.vector.tensor_copy(out=position[:], in_=position_i32[:])
-        table = const.tile([P, T, 3 * PAIRS], F32)
-        angles(0)
-        sines(0)
-        angles(1)
+        quarter_turn = const.tile([P, 1], F32)
+        nc.vector.tensor_scalar_mul(out=quarter_turn[:], in0=one[:], scalar1=math.pi / 2)
 
         even_then_odd = const.tile([P, P], F32)
-        nc.vector.tensor_copy(
+        nc.scalar.copy(
             out=even_then_odd[:].rearrange("p (h e i) -> p h e i", h=H, e=2),
             in_=identity[:].rearrange("p (h i e) -> p h e i", h=H, e=2),
         )
         bias_f32 = const.tile([P, 1], F32)
-        nc.vector.tensor_copy(out=bias_f32[:], in_=bias_bf16[:])
+        nc.scalar.copy(out=bias_f32[:], in_=bias_bf16[:])
+
+        table = const.tile([P, T, 3 * PAIRS], F32)
+        angles((0, 1))
+        sine(0)
+        cosine(0)
 
         w_grouped = const.tile([P, PASSES, P, PACK], BF16, align_bytes=64)
         flip_rows(w_sb[:].bitcast(F32), w_grouped[:].bitcast(F32), by_vector=False)
@@ -254,22 +285,39 @@ def tile_weightlinearattention_pa_t_kernel(tc, x, w, bias, out):
             scales=w_scales[:],
             in_=w_grouped[:].rearrange("p g r v -> p (g r v)"),
         )
-        for r in range(GROUPS + 4):
+
+        for r in range(GROUPS):
             if 0 < r <= GROUPS - PREFETCH:
                 load(r - 1 + PREFETCH)
-            if 0 <= r - 2 < GROUPS:
+            if r >= 2:
                 quantise(r - 2)
-            if r < GROUPS:
-                flip_group(r)
-            if 0 <= r - 3 < GROUPS:
+            flip_group(r)
+            if r >= 3:
                 flip_back(r - 3)
-            if 0 <= r - 2 < GROUPS:
+            if r >= 2:
                 project(r - 2)
-            if r - 4 >= 0:
-                rotate(r - 4, nc.vector if r - 4 >= GROUPS - 4 else nc.gpsimd)
+            if r >= 4:
+                rotate(r - 4, nc.gpsimd if r - 4 < GPSIMD_ADDS else nc.vector)
             if r == 1:
-                sines(1)
-            if r == 2:
-                angles(2)
-            if r == 3:
-                sines(2)
+                sine(1)
+                cosine(1)
+                negate(0)
+                negate(1)
+                angles((2,))
+            if r == 6:
+                sine(2)
+            if r == 8:
+                minus_sine(2)
+            if r == 10:
+                cosine(2)
+
+        quantise(GROUPS - 2)
+        quantise(GROUPS - 1)
+        flip_back(GROUPS - 3)
+        project(GROUPS - 2)
+        project(GROUPS - 1)
+        rotate(GROUPS - 4, nc.vector)
+        flip_back(GROUPS - 2)
+        flip_back(GROUPS - 1)
+        for g in range(GROUPS - 3, GROUPS):
+            rotate(g, nc.vector)

@@ -31,11 +31,11 @@ N_MAX = max(GROUP_T) * B * P
 PLANES = B * H
 STORE_T = (8, 8, 8, 4, 2, 1, 1)
 STORE_ENDS = tuple(sum(STORE_T[: s + 1]) for s in range(len(STORE_T)))
-PREFETCH = 7
+PREFETCH = 9
 TABLE_T = (8, 8, 16)
 TABLE_FIRST = tuple(sum(TABLE_T[:c]) for c in range(len(TABLE_T)))
 
-SIN, COS, MINUS_SIN = 0, PAIRS, 2 * PAIRS
+SIN, COS, MINUS_SIN, COS2 = (1, 0), (0, 0), (0, 1), (1, 1)
 GPSIMD_ADDS = GROUPS - 6
 
 ROUND_MAGIC = 1.5 * 2.0**23
@@ -59,7 +59,7 @@ def tile_weightlinearattention_pa_t_kernel(tc, x, w, bias, out):
         tc.psum_pool(name="tokens", bufs=2) as tokens_pool,
     ):
         x_tiles, codes_tiles, scales_tiles, grouped_tiles, relu_tiles, token_tiles = {}, {}, {}, {}, {}, {}
-        result_tiles, turns_tiles, whole_tiles, fraction_tiles, folded_tiles = {}, {}, {}, {}, {}
+        product_tiles, result_tiles, turns_tiles, whole_tiles, fraction_tiles, folded_tiles = {}, {}, {}, {}, {}, {}
 
         def load(g):
             x_sb = loads.tile([P, GROUP_T[g], B, E], BF16)
@@ -125,21 +125,23 @@ def tile_weightlinearattention_pa_t_kernel(tc, x, w, bias, out):
                 nc.tensor.transpose(tokens[:, block], relu_tiles[g][:, block], even_then_odd[:])
             token_tiles[g] = tokens
 
-        def rotate(g, add_engine):
+        def multiply(g):
             first, size = FIRST_T[g], GROUP_T[g]
             n = size * B * P
-            shape = [P, size, PLANES, D]
+            shape = [P, size, PLANES, 2, D]
             tokens = token_tiles[g][:, :n].rearrange("p (t q d) -> p t q d", t=size, q=PLANES)
-            products = work.tile([P, 2, n], F32)
-            for a in range(2):
-                column = (COS, SIN)[a]
-                factors = table[:, first : first + size, column : column + D]
-                nc.vector.tensor_tensor(
-                    out=products[:, a, :].rearrange("p (t q d) -> p t q d", t=size, q=PLANES),
-                    in0=tokens,
-                    in1=factors.unsqueeze(2).to_broadcast(shape),
-                    op=ALU.mult,
-                )
+            products = work.tile([P, size, PLANES, 2, D], F32)
+            nc.vector.tensor_tensor(
+                out=products[:],
+                in0=tokens.unsqueeze(3).to_broadcast(shape),
+                in1=table[:, first : first + size].unsqueeze(2).to_broadcast(shape),
+                op=ALU.mult,
+            )
+            product_tiles[g] = products
+
+        def add_terms(g, engine):
+            first, size = FIRST_T[g], GROUP_T[g]
+            products = product_tiles[g]
             s = min(i for i in range(len(STORE_T)) if first < STORE_ENDS[i])
             store_first = STORE_ENDS[s] - STORE_T[s]
             if first == store_first:
@@ -147,8 +149,8 @@ def tile_weightlinearattention_pa_t_kernel(tc, x, w, bias, out):
                 result_tiles[s] = result
             result = result_tiles[s]
             local = first - store_first
-            terms = products[:].rearrange("p a (t q e i) -> p e t q i a", t=size, q=PLANES, e=2)
-            add_engine.tensor_tensor(
+            terms = products[:].rearrange("p t q a (e i) -> p e t q i a", e=2)
+            engine.tensor_tensor(
                 out=result[:, :, local : local + size, :].rearrange("p q t (i a) -> p t q i a", a=2),
                 in0=terms[:, 0],
                 in1=terms[:, 1],
@@ -199,7 +201,8 @@ def tile_weightlinearattention_pa_t_kernel(tc, x, w, bias, out):
                 folded_tiles[c] = folded
 
         def table_part(c, column):
-            return table[:, TABLE_FIRST[c] : TABLE_FIRST[c] + TABLE_T[c], column : column + PAIRS]
+            a, e = column
+            return table[:, TABLE_FIRST[c] : TABLE_FIRST[c] + TABLE_T[c], a, e * PAIRS : (e + 1) * PAIRS]
 
         def sine(c):
             nc.scalar.activation(
@@ -213,6 +216,11 @@ def tile_weightlinearattention_pa_t_kernel(tc, x, w, bias, out):
                 func=ACT.Sin,
                 bias=quarter_turn[:],
                 scale=2 * math.pi,
+            )
+
+        def copy_cosine(c):
+            nc.gpsimd.tensor_scalar(
+                out=table_part(c, COS2), in0=table_part(c, COS), scalar1=1.0, scalar2=0.0, op0=ALU.mult, op1=ALU.add
             )
 
         def minus_sine(c):
@@ -271,10 +279,12 @@ def tile_weightlinearattention_pa_t_kernel(tc, x, w, bias, out):
         bias_f32 = const.tile([P, 1], F32)
         nc.scalar.copy(out=bias_f32[:], in_=bias_bf16[:])
 
-        table = const.tile([P, T, 3 * PAIRS], F32)
+        table = const.tile([P, T, 2, D], F32)
         angles((0, 1))
         sine(0)
         cosine(0)
+
+        angles((2,))
 
         w_grouped = const.tile([P, PASSES, P, PACK], BF16, align_bytes=64)
         flip_rows(w_sb[:].bitcast(F32), w_grouped[:].bitcast(F32), by_vector=False)
@@ -297,27 +307,36 @@ def tile_weightlinearattention_pa_t_kernel(tc, x, w, bias, out):
             if r >= 2:
                 project(r - 2)
             if r >= 4:
-                rotate(r - 4, nc.gpsimd if r - 4 < GPSIMD_ADDS else nc.vector)
+                multiply(r - 4)
+                add_terms(r - 4, nc.gpsimd if r - 4 < GPSIMD_ADDS else nc.vector)
             if r == 1:
                 sine(1)
                 cosine(1)
                 negate(0)
                 negate(1)
-                angles((2,))
+                copy_cosine(0)
+                copy_cosine(1)
             if r == 6:
                 sine(2)
             if r == 8:
                 minus_sine(2)
             if r == 10:
                 cosine(2)
+            if r == 11:
+                nc.scalar.copy(out=table_part(2, COS2), in_=table_part(2, COS))
 
         quantise(GROUPS - 2)
         quantise(GROUPS - 1)
         flip_back(GROUPS - 3)
         project(GROUPS - 2)
         project(GROUPS - 1)
-        rotate(GROUPS - 4, nc.vector)
+        multiply(GROUPS - 4)
+        add_terms(GROUPS - 4, nc.gpsimd)
         flip_back(GROUPS - 2)
+        multiply(GROUPS - 3)
         flip_back(GROUPS - 1)
-        for g in range(GROUPS - 3, GROUPS):
-            rotate(g, nc.vector)
+        multiply(GROUPS - 2)
+        add_terms(GROUPS - 3, nc.vector)
+        multiply(GROUPS - 1)
+        add_terms(GROUPS - 2, nc.gpsimd)
+        add_terms(GROUPS - 1, nc.vector)

import math

import concourse.mybir as mybir
from concourse.masks import make_identity

F32 = mybir.dt.float32
BF16 = mybir.dt.bfloat16
I32 = mybir.dt.int32
U32 = mybir.dt.uint32
U8 = mybir.dt.uint8
FP8X4 = mybir.dt.float8_e4m3fn_x4
ALU = mybir.AluOpType
ACT = mybir.ActivationFunctionType

P = 128
L, B, E, H, D = 4096, 2, 1024, 2, 64
PAIRS = D // 2
FLOPS = 2 * L * B * E * H * D

PACK = 4
K_PASS = P * PACK
PASSES = E // K_PASS
WORDS = E // 2
TRANSPOSES = WORDS // P

T = L // P
GROUP_T = (1, 1) + (2,) * 14 + (1, 1)
GROUPS = len(GROUP_T)
FIRST_T = tuple(sum(GROUP_T[:g]) for g in range(GROUPS))
N_MAX = max(GROUP_T) * B * P
PLANES = B * H
STORE_T = (8, 8, 8, 4, 2, 1, 1)
STORE_ENDS = tuple(sum(STORE_T[: s + 1]) for s in range(len(STORE_T)))
PREFETCH = 9
TABLE_T = (8, 8, 16)
TABLE_FIRST = tuple(sum(TABLE_T[:c]) for c in range(len(TABLE_T)))

SIN, COS, MINUS_SIN, COS2 = (1, 0), (0, 0), (0, 1), (1, 1)
GPSIMD_ADDS = GROUPS - 6

ROUND_MAGIC = 1.5 * 2.0**23
DIRECT_THETAS = 8


def tile_weightlinearattention_pa_t_kernel(tc, x, w, bias, out):
    nc = tc.nc
    x_rows = x.rearrange("(p t) c k -> p t c k", t=T)
    out_rows = out.rearrange("c h (p t) d -> p (c h) t d", t=T)

    with (
        tc.manual_schedule(),
        tc.tile_pool(name="const", bufs=1) as const,
        tc.tile_pool(name="loads", bufs=PREFETCH + 1) as loads,
        tc.tile_pool(name="work", bufs=3) as work,
        tc.tile_pool(name="results", bufs=5) as results,
        tc.tile_pool(name="grouped", bufs=4) as groupeds,
        tc.psum_pool(name="flipped", bufs=4) as flipped_pool,
        tc.psum_pool(name="sums", bufs=2) as sums_pool,
        tc.psum_pool(name="tokens", bufs=2) as tokens_pool,
    ):
        x_tiles, codes_tiles, scales_tiles, grouped_tiles, relu_tiles, token_tiles = {}, {}, {}, {}, {}, {}
        product_tiles, result_tiles, turns_tiles, whole_tiles, fraction_tiles, folded_tiles = {}, {}, {}, {}, {}, {}

        def load(g):
            x_sb = loads.tile([P, GROUP_T[g], B, E], BF16)
            nc.sync.dma_start(out=x_sb[:], in_=x_rows[:, FIRST_T[g] : FIRST_T[g] + GROUP_T[g]])
            x_tiles[g] = x_sb

        def flip_rows(words, grouped_words, by_vector):
            flipped = flipped_pool.tile([P, TRANSPOSES, P], F32)
            for j in range(TRANSPOSES):
                nc.tensor.transpose(flipped[:, j, :], words[:, j * P : (j + 1) * P], identity[:])
            side_by_side = flipped[:].rearrange("p (g u) r -> p g r u", g=PASSES)
            if by_vector:
                nc.vector.tensor_copy(out=grouped_words, in_=side_by_side)
            else:
                nc.scalar.copy(out=grouped_words, in_=side_by_side)

        def flip_group(g):
            words = x_tiles[g][:].bitcast(F32)
            blocks = GROUP_T[g] * B
            grouped = groupeds.tile([P, PASSES, blocks, P, PACK], BF16, align_bytes=64)
            for t in range(GROUP_T[g]):
                for c in range(B):
                    b = t * B + c
                    flip_rows(
                        words[:, t, c, :],
                        grouped[:].bitcast(F32)[:, :, b, :, :],
                        by_vector=(b == 0 and GROUP_T[g] == 2),
                    )
            grouped_tiles[g] = grouped

        def quantise(g):
            n = GROUP_T[g] * B * P
            codes = work.tile([P, PASSES * n], U32, align_bytes=64)
            scales = work.tile([P, PASSES * n], U8, align_bytes=64)
            nc.vector.quantize_mx(
                out=codes[:].bitcast(FP8X4),
                scales=scales[:],
                in_=grouped_tiles[g][:].rearrange("p g b r v -> p (g b r v)"),
            )
            codes_tiles[g], scales_tiles[g] = codes, scales

        def project(g):
            n = GROUP_T[g] * B * P
            sums = sums_pool.tile([P, N_MAX], F32)
            for k in range(PASSES):
                nc.tensor.matmul_mx(
                    out=sums[:, :n],
                    lhsT=w_codes[:, k * P : (k + 1) * P].bitcast(FP8X4),
                    lhsT_scale=w_scales[:, k * P : (k + 1) * P],
                    rhs=codes_tiles[g][:, k * n : (k + 1) * n].bitcast(FP8X4),
                    rhs_scale=scales_tiles[g][:, k * n : (k + 1) * n],
                    start=(k == 0),
                    stop=(k == PASSES - 1),
                )
            relu = work.tile([P, n], F32)
            nc.scalar.activation(out=relu[:], in_=sums[:, :n], func=ACT.Relu, bias=bias_f32[:], scale=1.0)
            relu_tiles[g] = relu

        def flip_back(g):
            tokens = tokens_pool.tile([P, N_MAX], F32)
            for b in range(GROUP_T[g] * B):
                block = slice(b * P, (b + 1) * P)
                nc.tensor.transpose(tokens[:, block], relu_tiles[g][:, block], even_then_odd[:])
            token_tiles[g] = tokens

        def multiply(g):
            first, size = FIRST_T[g], GROUP_T[g]
            n = size * B * P
            shape = [P, size, PLANES, 2, D]
            tokens = token_tiles[g][:, :n].rearrange("p (t q d) -> p t q d", t=size, q=PLANES)
            products = work.tile([P, size, PLANES, 2, D], F32)
            nc.vector.tensor_tensor(
                out=products[:],
                in0=tokens.unsqueeze(3).to_broadcast(shape),
                in1=table[:, first : first + size].unsqueeze(2).to_broadcast(shape),
                op=ALU.mult,
            )
            product_tiles[g] = products

        def add_terms(g, engine):
            first, size = FIRST_T[g], GROUP_T[g]
            products = product_tiles[g]
            s = min(i for i in range(len(STORE_T)) if first < STORE_ENDS[i])
            store_first = STORE_ENDS[s] - STORE_T[s]
            if first == store_first:
                result = results.tile([P, PLANES, STORE_T[s], D], F32)
                result_tiles[s] = result
            result = result_tiles[s]
            local = first - store_first
            terms = products[:].rearrange("p t q a (e i) -> p e t q i a", e=2)
            engine.tensor_tensor(
                out=result[:, :, local : local + size, :].rearrange("p q t (i a) -> p t q i a", a=2),
                in0=terms[:, 0],
                in1=terms[:, 1],
                op=ALU.add,
            )
            if first + size == STORE_ENDS[s]:
                nc.sync.dma_start(out=out_rows[:, :, store_first : STORE_ENDS[s], :], in_=result[:])

        def angles(parts):
            for c in parts:
                first, size = TABLE_FIRST[c], TABLE_T[c]
                shape = [P, size, PAIRS]
                turns = work.tile([P, size, PAIRS], F32)
                nc.vector.tensor_tensor(
                    out=turns[:],
                    in0=position[:, first : first + size].unsqueeze(2).to_broadcast(shape),
                    in1=theta[:].unsqueeze(1).to_broadcast(shape),
                    op=ALU.mult,
                )
                turns_tiles[c] = turns
            for c in parts:
                whole_turns = work.tile([P, TABLE_T[c], PAIRS], F32)
                nc.vector.tensor_scalar(
                    out=whole_turns[:],
                    in0=turns_tiles[c][:],
                    scalar1=ROUND_MAGIC,
                    scalar2=ROUND_MAGIC,
                    op0=ALU.add,
                    op1=ALU.subtract,
                )
                whole_tiles[c] = whole_turns
            for c in parts:
                fraction = work.tile([P, TABLE_T[c], PAIRS], F32)
                nc.vector.tensor_tensor(
                    out=fraction[:], in0=turns_tiles[c][:], in1=whole_tiles[c][:], op=ALU.subtract
                )
                fraction_tiles[c] = fraction
            for c in parts:
                folded = work.tile([P, TABLE_T[c], PAIRS], F32)
                nc.vector.scalar_tensor_tensor(
                    out=folded[:],
                    in0=fraction_tiles[c][:],
                    scalar=-1.0,
                    in1=fraction_tiles[c][:],
                    op0=ALU.mult,
                    op1=ALU.min,
                )
                folded_tiles[c] = folded

        def table_part(c, column):
            a, e = column
            return table[:, TABLE_FIRST[c] : TABLE_FIRST[c] + TABLE_T[c], a, e * PAIRS : (e + 1) * PAIRS]

        def sine(c):
            nc.scalar.activation(
                out=table_part(c, SIN), in_=fraction_tiles[c][:], func=ACT.Sin, scale=2 * math.pi
            )

        def cosine(c):
            nc.scalar.activation(
                out=table_part(c, COS),
                in_=folded_tiles[c][:],
                func=ACT.Sin,
                bias=quarter_turn[:],
                scale=2 * math.pi,
            )

        def copy_cosine(c):
            nc.gpsimd.tensor_scalar(
                out=table_part(c, COS2), in0=table_part(c, COS), scalar1=1.0, scalar2=0.0, op0=ALU.mult, op1=ALU.add
            )

        def minus_sine(c):
            nc.scalar.activation(
                out=table_part(c, MINUS_SIN), in_=fraction_tiles[c][:], func=ACT.Sin, scale=-2 * math.pi
            )

        def negate(c):
            nc.gpsimd.tensor_scalar(
                out=table_part(c, MINUS_SIN),
                in0=table_part(c, SIN),
                scalar1=-1.0,
                scalar2=0.0,
                op0=ALU.mult,
                op1=ALU.add,
            )

        w_sb = const.tile([P, E], BF16)
        nc.sync.dma_start(out=w_sb[:], in_=w)
        for g in range(PREFETCH):
            load(g)
        bias_bf16 = const.tile([P, 1], BF16)
        nc.scalar.dma_start(out=bias_bf16[:], in_=bias.rearrange("(f o) -> f o", o=1))

        position_i32 = const.tile([P, T], I32)
        nc.gpsimd.iota(position_i32[:], pattern=[[1, T]], base=0, channel_multiplier=T)
        identity = const.tile([P, P], F32)
        make_identity(nc, identity[:])

        one = const.tile([P, 1], F32)
        nc.vector.memset(one[:], 1.0)
        first_sine = const.tile([P, 1], F32)
        nc.scalar.activation(out=first_sine[:], in_=one[:], func=ACT.Sin)

        theta = const.tile([P, PAIRS], F32)
        for i in range(DIRECT_THETAS):
            nc.vector.tensor_scalar_mul(
                out=theta[:, i : i + 1], in0=one[:], scalar1=10000.0 ** (-2.0 * i / D) / (2 * math.pi)
            )
        made = DIRECT_THETAS
        while made < PAIRS:
            nc.vector.tensor_scalar_mul(
                out=theta[:, made : 2 * made], in0=theta[:, :made], scalar1=10000.0 ** (-2.0 * made / D)
            )
            made = 2 * made
        position = const.tile([P, T], F32)
        nc.vector.tensor_copy(out=position[:], in_=position_i32[:])
        quarter_turn = const.tile([P, 1], F32)
        nc.vector.tensor_scalar_mul(out=quarter_turn[:], in0=one[:], scalar1=math.pi / 2)

        even_then_odd = const.tile([P, P], F32)
        nc.scalar.copy(
            out=even_then_odd[:].rearrange("p (h e i) -> p h e i", h=H, e=2),
            in_=identity[:].rearrange("p (h i e) -> p h e i", h=H, e=2),
        )
        bias_f32 = const.tile([P, 1], F32)
        nc.scalar.copy(out=bias_f32[:], in_=bias_bf16[:])

        table = const.tile([P, T, 2, D], F32)
        angles((0, 1))
        sine(0)
        cosine(0)

        angles((2,))

        w_grouped = const.tile([P, PASSES, P, PACK], BF16, align_bytes=64)
        flip_rows(w_sb[:].bitcast(F32), w_grouped[:].bitcast(F32), by_vector=False)
        w_codes = const.tile([P, PASSES * P], U32, align_bytes=64)
        w_scales = const.tile([P, PASSES * P], U8, align_bytes=64)
        nc.vector.quantize_mx(
            out=w_codes[:].bitcast(FP8X4),
            scales=w_scales[:],
            in_=w_grouped[:].rearrange("p g r v -> p (g r v)"),
        )

        for r in range(GROUPS):
            if 0 < r <= GROUPS - PREFETCH:
                load(r - 1 + PREFETCH)
            if r >= 2:
                quantise(r - 2)
            flip_group(r)
            if r >= 3:
                flip_back(r - 3)
            if r >= 2:
                project(r - 2)
            if r >= 4:
                multiply(r - 4)
                add_terms(r - 4, nc.gpsimd if r - 4 < GPSIMD_ADDS else nc.vector)
            if r == 1:
                sine(1)
                cosine(1)
                negate(0)
                negate(1)
                copy_cosine(0)
                copy_cosine(1)
            if r == 6:
                sine(2)
            if r == 8:
                minus_sine(2)
            if r == 10:
                cosine(2)
            if r == 11:
                nc.scalar.copy(out=table_part(2, COS2), in_=table_part(2, COS))

        quantise(GROUPS - 2)
        quantise(GROUPS - 1)
        flip_back(GROUPS - 3)
        project(GROUPS - 2)
        project(GROUPS - 1)
        multiply(GROUPS - 4)
        add_terms(GROUPS - 4, nc.gpsimd)
        flip_back(GROUPS - 2)
        multiply(GROUPS - 3)
        flip_back(GROUPS - 1)
        multiply(GROUPS - 2)
        add_terms(GROUPS - 3, nc.vector)
        multiply(GROUPS - 1)
        add_terms(GROUPS - 2, nc.gpsimd)
        add_terms(GROUPS - 1, nc.vector)
